import numpy as np
import ml_dtypes


def mxq(x, axis, fmt="e4m3"):
    dtype, down = {"e4m3": (ml_dtypes.float8_e4m3fn, 7), "e5m2": (ml_dtypes.float8_e5m2, 14)}[fmt]
    v = np.moveaxis(np.asarray(x, np.float32).astype(ml_dtypes.bfloat16).astype(np.float64), axis, -1)
    blocks = v.reshape(v.shape[:-1] + (-1, 32))
    amax = np.abs(blocks).max(-1, keepdims=True)
    byte = np.maximum(np.where(amax > 0, np.frexp(amax)[1] - 1 + 127, 0) - down, 1)
    scale = np.exp2(byte - 127.0)
    codes = (blocks / scale).astype(np.float32).astype(dtype).astype(np.float64)
    return np.moveaxis((codes * scale).reshape(v.shape), -1, axis)


WIDE = False


def mx_kscale(k):
    if not WIDE:
        return np.ones(k)
    levels = np.array([10, -10, 5, -5, 0])
    a = np.random.permutation(np.resize(levels, k // 512 * 4)).reshape(k // 512, 4)
    idx = np.arange(k)
    return np.exp2(a[idx // 512, idx % 128 // 32])


BF16 = ml_dtypes.bfloat16


def bf(x):
    return np.asarray(x, np.float32).astype(BF16)


def f64(x):
    return np.asarray(x).astype(np.float64)


B, I, H = 128, 256, 256
K = H + I
NAMES = ["w_f_light", "w_i_light", "w_c_light", "w_o_light",
         "w_f_light_temp", "w_i_light_temp", "w_c_light_temp", "w_o_light_temp"]


def sigmoid(v):
    return 1.0 / (1.0 + np.exp(-v))


def setup_inputs():
    s = mx_kscale(K)
    inp = {
        "y": bf(np.random.standard_normal((B, I)) * s[H:]),
        "h_light": bf(np.random.standard_normal((B, H)) * s[:H]),
        "c_light": bf(np.random.standard_normal((B, H))),
        "h_temp": bf(np.random.standard_normal((B, H)) * s[:H]),
        "c_temp": bf(np.random.standard_normal((B, H))),
    }
    for n in NAMES:
        inp[n] = bf(np.random.standard_normal((H, K)) / np.sqrt(K) / s)
        inp["b" + n[1:]] = bf(np.random.standard_normal(H) * 0.5)
    return inp


def _branch(hx, wf, b_f, wi, b_i, wc, b_c, wo, b_o):
    W = np.concatenate([wf, wi, wc, wo], axis=0)
    b = np.concatenate([b_f, b_i, b_c, b_o], axis=0)
    z = (mxq(hx, 1, "e4m3") @ mxq(W.T, 0, "e4m3")) + b
    zf, zi, zc, zo = np.split(z, 4, axis=1)
    return sigmoid(zf), sigmoid(zi), np.tanh(zc), sigmoid(zo)


def reference(y, h_light, c_light, h_temp, c_temp,
              w_f_light, b_f_light, w_i_light, b_i_light,
              w_c_light, b_c_light, w_o_light, b_o_light,
              w_f_light_temp, b_f_light_temp, w_i_light_temp, b_i_light_temp,
              w_c_light_temp, b_c_light_temp, w_o_light_temp, b_o_light_temp):
    y, h_light, c_light, h_temp = f64(y), f64(h_light), f64(c_light), f64(h_temp)
    hx_l = np.concatenate([h_light, y], axis=1)
    hx_t = np.concatenate([h_temp, y], axis=1)
    f1, i1, ch1, o1 = _branch(hx_l, f64(w_f_light), f64(b_f_light), f64(w_i_light), f64(b_i_light),
                              f64(w_c_light), f64(b_c_light), f64(w_o_light), f64(b_o_light))
    f2, i2, ch2, o2 = _branch(hx_t, f64(w_f_light_temp), f64(b_f_light_temp), f64(w_i_light_temp), f64(b_i_light_temp),
                              f64(w_c_light_temp), f64(b_c_light_temp), f64(w_o_light_temp), f64(b_o_light_temp))
    c_new = (f1 * c_light + i1 * ch1) + (f2 * c_light + i2 * ch2)
    h_new = (o1 + o2) * np.tanh(c_new)
    return h_new, c_new

@@ -1,0 +1,259 @@
+from contextlib import ExitStack
+
+import concourse.mybir as mybir
+from concourse.masks import make_identity
+
+BF16 = mybir.dt.bfloat16
+F32 = mybir.dt.float32
+U32 = mybir.dt.uint32
+U8 = mybir.dt.uint8
+FP8X4 = mybir.dt.float8_e4m3fn_x4
+ACT = mybir.ActivationFunctionType
+
+P = 128
+H = 256
+K = 2 * H
+BANK = 512
+BRANCHES = 2
+PARITIES = 2
+GATES = ("i", "c", "f", "o")
+GATE_FUNC = {"i": ACT.Sigmoid, "c": ACT.Tanh, "f": ACT.Sigmoid, "o": ACT.Sigmoid}
+
+FLOPS = 2 * P * K * len(GATES) * BRANCHES * H
+
+
+def tile_customlstmcell_s_kernel(
+    tc,
+    y,
+    h_light,
+    c_light,
+    h_temp,
+    c_temp,
+    w_f_light,
+    b_f_light,
+    w_i_light,
+    b_i_light,
+    w_c_light,
+    b_c_light,
+    w_o_light,
+    b_o_light,
+    w_f_light_temp,
+    b_f_light_temp,
+    w_i_light_temp,
+    b_i_light_temp,
+    w_c_light_temp,
+    b_c_light_temp,
+    w_o_light_temp,
+    b_o_light_temp,
+    out_0,
+    out_1,
+):
+    nc = tc.nc
+    weight_of = {
+        "f": (w_f_light, w_f_light_temp),
+        "i": (w_i_light, w_i_light_temp),
+        "c": (w_c_light, w_c_light_temp),
+        "o": (w_o_light, w_o_light_temp),
+    }
+    bias_of = {
+        "f": (b_f_light, b_f_light_temp),
+        "i": (b_i_light, b_i_light_temp),
+        "c": (b_c_light, b_c_light_temp),
+        "o": (b_o_light, b_o_light_temp),
+    }
+
+    with ExitStack() as ctx:
+        keep = ctx.enter_context(tc.tile_pool(name="keep", bufs=1))
+        flipped = ctx.enter_context(tc.psum_pool(name="flipped", bufs=4))
+        sums = ctx.enter_context(tc.psum_pool(name="sums", bufs=4))
+        ctx.enter_context(tc.manual_schedule())
+
+        ident = keep.tile([P, P], F32, name="ident")
+        make_identity(nc, ident[:])
+        bias_rows = [keep.tile([P, H], BF16, name="bias_rows_%d" % half) for half in range(2)]
+        for half in range(2):
+            nc.vector.memset(bias_rows[half][:], 0.0)
+        warm_in = keep.tile([P, 1], F32, name="warm_in")
+        warm_out = keep.tile([P, 1], F32, name="warm_out")
+        nc.vector.memset(warm_in[:], 0.0)
+        nc.scalar.activation(out=warm_out[:], in_=warm_in[:], func=ACT.Sigmoid)
+
+        hl_sb = keep.tile([P, H], BF16, name="hl_sb")
+        y_sb = keep.tile([P, H], BF16, name="y_sb")
+        ht_sb = keep.tile([P, H], BF16, name="ht_sb")
+        cl_sb = keep.tile([P, H], BF16, name="cl_sb")
+        w_sb = {}
+        for gate in GATES:
+            for branch in range(BRANCHES):
+                w_sb[gate, branch] = keep.tile([P, PARITIES * K], BF16, name="w_%s%d" % (gate, branch))
+
+        def load_weights(gate):
+            for branch in range(BRANCHES):
+                nc.sync.dma_start(
+                    out=w_sb[gate, branch][:],
+                    in_=weight_of[gate][branch].rearrange("(m a) k -> m (a k)", a=PARITIES),
+                )
+
+        def load_biases(half):
+            for place, gate in enumerate(GATES[2 * half : 2 * half + 2]):
+                for branch in range(BRANCHES):
+                    row = BRANCHES * place + branch
+                    nc.sync.dma_start(
+                        out=bias_rows[half][row : row + 1, :],
+                        in_=bias_of[gate][branch].rearrange("(o n) -> o n", o=1),
+                    )
+
+        nc.sync.dma_start(out=hl_sb[:], in_=h_light)
+        nc.sync.dma_start(out=y_sb[:], in_=y)
+        nc.sync.dma_start(out=ht_sb[:], in_=h_temp)
+        nc.sync.dma_start(out=cl_sb[:], in_=c_light)
+        load_weights("i")
+        load_weights("c")
+        load_biases(0)
+        load_weights("f")
+        load_weights("o")
+        load_biases(1)
+
+        def transpose_words(bank, place, tile_bf16, first_word):
+            nc.tensor.transpose(
+                bank[:, place * P : (place + 1) * P],
+                tile_bf16[:].bitcast(F32)[:, first_word : first_word + P],
+                ident[:],
+            )
+
+        def regroup(on_scalar, grouped, bank):
+            src = bank[:].rearrange("q (g u r) -> q g r u", g=2, u=2)
+            dst = grouped[:].bitcast(F32).rearrange("q (g r u) -> q g r u", g=2, u=2)
+            if on_scalar:
+                nc.scalar.copy(out=dst, in_=src)
+            else:
+                nc.vector.tensor_copy(out=dst, in_=src)
+
+        hx_bank = flipped.tile([P, BANK], F32, name="bank", tag="bank")
+        for place, tile_bf16 in enumerate((hl_sb, y_sb, ht_sb, y_sb)):
+            transpose_words(hx_bank, place, tile_bf16, 0)
+        hx_grouped = keep.tile([P, BRANCHES * P * 4], BF16, name="hx_grouped", align_bytes=64)
+        regroup(True, hx_grouped, hx_bank)
+
+        cl_bank = flipped.tile([P, BANK], F32, name="bank", tag="bank")
+        transpose_words(cl_bank, 0, cl_sb, 0)
+        c_old = keep.tile([P, H], F32, name="c_old")
+        nc.scalar.copy(
+            out=c_old[:].rearrange("m (a b) -> m a b", a=PARITIES),
+            in_=cl_bank[:, 0:P].bitcast(BF16).rearrange("m (b a) -> m a b", a=PARITIES),
+        )
+
+        hx_codes = keep.tile([P, BRANCHES * P], U32, name="hx_codes", align_bytes=64)
+        hx_scales = keep.tile([P, BRANCHES * P], U8, name="hx_scales", align_bytes=64)
+        nc.vector.quantize_mx(out=hx_codes[:].bitcast(FP8X4), scales=hx_scales[:], in_=hx_grouped[:])
+
+        grouped = {}
+        w_codes = keep.tile([P, len(GATES) * BRANCHES, H], U32, name="w_codes", align_bytes=64)
+        w_scales = keep.tile([P, len(GATES) * BRANCHES, H], U8, name="w_scales", align_bytes=64)
+        bias = keep.tile([P, len(GATES) * BRANCHES * PARITIES], F32, name="bias")
+        gate_sb = {}
+        for gate in GATES:
+            gate_sb[gate] = keep.tile([P, BRANCHES * H], F32, name="gate_%s" % gate)
+
+        def flip_weights(gate):
+            for branch in range(BRANCHES):
+                bank = flipped.tile([P, BANK], F32, name="bank", tag="bank")
+                for place in range(4):
+                    transpose_words(bank, place, w_sb[gate, branch], place * P)
+                grouped[gate, branch] = keep.tile(
+                    [P, H * 4], BF16, name="grouped_%s%d" % (gate, branch), align_bytes=64
+                )
+                regroup(branch == 0, grouped[gate, branch], bank)
+
+        def flip_biases(half):
+            bank = flipped.tile([P, BANK], F32, name="bank", tag="bank")
+            transpose_words(bank, 0, bias_rows[half], 0)
+            nc.scalar.copy(out=bias[:, 8 * half : 8 * half + 8], in_=bank[:, 0:4].bitcast(BF16))
+
+        def quantise_weights(gate):
+            for branch in range(BRANCHES):
+                slot = BRANCHES * GATES.index(gate) + branch
+                nc.vector.quantize_mx(
+                    out=w_codes[:, slot, :].bitcast(FP8X4),
+                    scales=w_scales[:, slot, :],
+                    in_=grouped[gate, branch][:],
+                )
+
+        def gate_values(gate):
+            z = {}
+            for branch in range(BRANCHES):
+                slot = BRANCHES * GATES.index(gate) + branch
+                z[branch] = sums.tile([P, H], F32, name="z", tag="z")
+                for parity in range(PARITIES):
+                    nc.tensor.matmul_mx(
+                        out=z[branch][:, parity * P : (parity + 1) * P],
+                        lhsT=w_codes[:, slot, parity * P : (parity + 1) * P].bitcast(FP8X4),
+                        lhsT_scale=w_scales[:, slot, parity * P : (parity + 1) * P],
+                        rhs=hx_codes[:, branch * P : (branch + 1) * P].bitcast(FP8X4),
+                        rhs_scale=hx_scales[:, branch * P : (branch + 1) * P],
+                        start=True,
+                        stop=True,
+                    )
+            for branch in range(BRANCHES):
+                slot = BRANCHES * GATES.index(gate) + branch
+                for parity in range(PARITIES):
+                    column = PARITIES * slot + parity
+                    nc.scalar.activation(
+                        out=gate_sb[gate][:, column % 4 * P : (column % 4 + 1) * P],
+                        in_=z[branch][:, parity * P : (parity + 1) * P],
+                        func=GATE_FUNC[gate],
+                        bias=bias[:, column : column + 1],
+                    )
+
+        def both(name):
+            return keep.tile([P, H], F32, name=name)
+
+        def store_transposed(dram, value, name):
+            bank = flipped.tile([P, BANK], F32, name="bank", tag="bank")
+            for parity in range(PARITIES):
+                nc.tensor.transpose(
+                    bank[:, parity * P : (parity + 1) * P], value[:, parity * P : (parity + 1) * P], ident[:]
+                )
+            rows = keep.tile([P, H], F32, name=name)
+            nc.scalar.copy(
+                out=rows[:].rearrange("b (m a) -> b m a", a=PARITIES),
+                in_=bank[:, 0:H].rearrange("b (a m) -> b m a", a=PARITIES),
+            )
+            nc.sync.dma_start(out=dram, in_=rows[:])
+
+        flip_weights("i")
+        quantise_weights("i")
+
+        flip_weights("c")
+        flip_biases(0)
+        gate_values("i")
+        quantise_weights("c")
+
+        flip_weights("f")
+        gate_values("c")
+        quantise_weights("f")
+        products = keep.tile([P, BRANCHES * H], F32, name="products")
+        nc.vector.tensor_mul(out=products[:], in0=gate_sb["i"][:], in1=gate_sb["c"][:])
+        written = both("written")
+        nc.vector.tensor_add(out=written[:], in0=products[:, 0:H], in1=products[:, H : 2 * H])
+
+        flip_weights("o")
+        flip_biases(1)
+        gate_values("f")
+        quantise_weights("o")
+        f_sum = both("f_sum")
+        nc.vector.tensor_add(out=f_sum[:], in0=gate_sb["f"][:, 0:H], in1=gate_sb["f"][:, H : 2 * H])
+        kept = both("kept")
+        nc.vector.tensor_mul(out=kept[:], in0=f_sum[:], in1=c_old[:])
+        c_new = both("c_new")
+        nc.vector.tensor_add(out=c_new[:], in0=kept[:], in1=written[:])
+
+        gate_values("o")
+        tanh_c = both("tanh_c")
+        nc.scalar.activation(out=tanh_c[:], in_=c_new[:], func=ACT.Tanh)
+        store_transposed(out_1, c_new, "c_rows")
+        o_sum = both("o_sum")
+        nc.vector.tensor_add(out=o_sum[:], in0=gate_sb["o"][:, 0:H], in1=gate_sb["o"][:, H : 2 * H])
+        h_new = both("h_new")
+        nc.vector.tensor_mul(out=h_new[:], in0=o_sum[:], in1=tanh_c[:])
+        store_transposed(out_0, h_new, "h_rows")

@@ -13,7 +13,6 @@ ACT = mybir.ActivationFunctionType
 P = 128
 H = 256
 K = 2 * H
-BANK = 512
 BRANCHES = 2
 PARITIES = 2
 GATES = ("i", "c", "f", "o")
@@ -65,7 +64,8 @@ def tile_customlstmcell_s_kernel(
     with ExitStack() as ctx:
         keep = ctx.enter_context(tc.tile_pool(name="keep", bufs=1))
         flipped = ctx.enter_context(tc.psum_pool(name="flipped", bufs=4))
-        sums = ctx.enter_context(tc.psum_pool(name="sums", bufs=4))
+        sums = ctx.enter_context(tc.psum_pool(name="sums", bufs=2))
+        totals = ctx.enter_context(tc.psum_pool(name="totals", bufs=1))
         ctx.enter_context(tc.manual_schedule())
 
         ident = keep.tile([P, P], F32, name="ident")
@@ -106,154 +106,177 @@ def tile_customlstmcell_s_kernel(
         nc.sync.dma_start(out=hl_sb[:], in_=h_light)
         nc.sync.dma_start(out=y_sb[:], in_=y)
         nc.sync.dma_start(out=ht_sb[:], in_=h_temp)
-        nc.sync.dma_start(out=cl_sb[:], in_=c_light)
         load_weights("i")
         load_weights("c")
         load_biases(0)
         load_weights("f")
         load_weights("o")
         load_biases(1)
+        nc.sync.dma_start(out=cl_sb[:], in_=c_light)
 
-        def transpose_words(bank, place, tile_bf16, first_word):
-            nc.tensor.transpose(
-                bank[:, place * P : (place + 1) * P],
-                tile_bf16[:].bitcast(F32)[:, first_word : first_word + P],
-                ident[:],
-            )
+        def words(tile_bf16, first_word):
+            return tile_bf16[:].bitcast(F32)[:, first_word : first_word + P]
 
-        def regroup(on_scalar, grouped, bank):
-            src = bank[:].rearrange("q (g u r) -> q g r u", g=2, u=2)
-            dst = grouped[:].bitcast(F32).rearrange("q (g r u) -> q g r u", g=2, u=2)
-            if on_scalar:
-                nc.scalar.copy(out=dst, in_=src)
-            else:
+        def flip(*sources):
+            bank = flipped.tile([P, 2 * P], F32, name="bank", tag="bank")
+            for u, source in enumerate(sources):
+                nc.tensor.transpose(bank[:, u * P : (u + 1) * P], source, ident[:])
+            return bank
+
+        def quantise(second, bank, codes, scales, name):
+            grouped = keep.tile([P, 4 * P], BF16, name=name, align_bytes=64)
+            src = bank[:].rearrange("q (u r) -> q r u", u=2)
+            dst = grouped[:].bitcast(F32).rearrange("q (r u) -> q r u", u=2)
+            if second:
                 nc.vector.tensor_copy(out=dst, in_=src)
+            else:
+                nc.scalar.copy(out=dst, in_=src)
+            return lambda: nc.vector.quantize_mx(out=codes.bitcast(FP8X4), scales=scales, in_=grouped[:])
 
-        hx_bank = flipped.tile([P, BANK], F32, name="bank", tag="bank")
-        for place, tile_bf16 in enumerate((hl_sb, y_sb, ht_sb, y_sb)):
-            transpose_words(hx_bank, place, tile_bf16, 0)
-        hx_grouped = keep.tile([P, BRANCHES * P * 4], BF16, name="hx_grouped", align_bytes=64)
-        regroup(True, hx_grouped, hx_bank)
-
-        cl_bank = flipped.tile([P, BANK], F32, name="bank", tag="bank")
-        transpose_words(cl_bank, 0, cl_sb, 0)
-        c_old = keep.tile([P, H], F32, name="c_old")
-        nc.scalar.copy(
-            out=c_old[:].rearrange("m (a b) -> m a b", a=PARITIES),
-            in_=cl_bank[:, 0:P].bitcast(BF16).rearrange("m (b a) -> m a b", a=PARITIES),
-        )
+        def halves(pair_of_sources, codes, scales, name):
+            pending = []
+            for second, sources in enumerate(pair_of_sources):
+                cols = slice(second * P, (second + 1) * P)
+                bank = flip(*sources)
+                pending.append(quantise(second, bank, codes[:, cols], scales[:, cols], "%s%d" % (name, second)))
+            for issue in pending:
+                issue()
 
         hx_codes = keep.tile([P, BRANCHES * P], U32, name="hx_codes", align_bytes=64)
         hx_scales = keep.tile([P, BRANCHES * P], U8, name="hx_scales", align_bytes=64)
-        nc.vector.quantize_mx(out=hx_codes[:].bitcast(FP8X4), scales=hx_scales[:], in_=hx_grouped[:])
+        halves(
+            ((words(hl_sb, 0), words(y_sb, 0)), (words(ht_sb, 0), words(y_sb, 0))),
+            hx_codes[:],
+            hx_scales[:],
+            "hx_grouped",
+        )
 
-        grouped = {}
         w_codes = keep.tile([P, len(GATES) * BRANCHES, H], U32, name="w_codes", align_bytes=64)
         w_scales = keep.tile([P, len(GATES) * BRANCHES, H], U8, name="w_scales", align_bytes=64)
         bias = keep.tile([P, len(GATES) * BRANCHES * PARITIES], F32, name="bias")
         gate_sb = {}
         for gate in GATES:
             gate_sb[gate] = keep.tile([P, BRANCHES * H], F32, name="gate_%s" % gate)
+        z = {}
 
-        def flip_weights(gate):
-            for branch in range(BRANCHES):
-                bank = flipped.tile([P, BANK], F32, name="bank", tag="bank")
-                for place in range(4):
-                    transpose_words(bank, place, w_sb[gate, branch], place * P)
-                grouped[gate, branch] = keep.tile(
-                    [P, H * 4], BF16, name="grouped_%s%d" % (gate, branch), align_bytes=64
-                )
-                regroup(branch == 0, grouped[gate, branch], bank)
+        def slot_of(gate, branch):
+            return BRANCHES * GATES.index(gate) + branch
+
+        def prepare(gate, branch):
+            tile_bf16 = w_sb[gate, branch]
+            slot = slot_of(gate, branch)
+            halves(
+                [(words(tile_bf16, parity * H), words(tile_bf16, parity * H + P)) for parity in range(PARITIES)],
+                w_codes[:, slot, :],
+                w_scales[:, slot, :],
+                "grouped_%s%d" % (gate, branch),
+            )
 
         def flip_biases(half):
-            bank = flipped.tile([P, BANK], F32, name="bank", tag="bank")
-            transpose_words(bank, 0, bias_rows[half], 0)
+            bank = flip(words(bias_rows[half], 0))
             nc.scalar.copy(out=bias[:, 8 * half : 8 * half + 8], in_=bank[:, 0:4].bitcast(BF16))
 
-        def quantise_weights(gate):
-            for branch in range(BRANCHES):
-                slot = BRANCHES * GATES.index(gate) + branch
-                nc.vector.quantize_mx(
-                    out=w_codes[:, slot, :].bitcast(FP8X4),
-                    scales=w_scales[:, slot, :],
-                    in_=grouped[gate, branch][:],
-                )
-
-        def gate_values(gate):
-            z = {}
-            for branch in range(BRANCHES):
-                slot = BRANCHES * GATES.index(gate) + branch
-                z[branch] = sums.tile([P, H], F32, name="z", tag="z")
-                for parity in range(PARITIES):
-                    nc.tensor.matmul_mx(
-                        out=z[branch][:, parity * P : (parity + 1) * P],
-                        lhsT=w_codes[:, slot, parity * P : (parity + 1) * P].bitcast(FP8X4),
-                        lhsT_scale=w_scales[:, slot, parity * P : (parity + 1) * P],
-                        rhs=hx_codes[:, branch * P : (branch + 1) * P].bitcast(FP8X4),
-                        rhs_scale=hx_scales[:, branch * P : (branch + 1) * P],
-                        start=True,
-                        stop=True,
-                    )
-            for branch in range(BRANCHES):
-                slot = BRANCHES * GATES.index(gate) + branch
-                for parity in range(PARITIES):
-                    column = PARITIES * slot + parity
-                    nc.scalar.activation(
-                        out=gate_sb[gate][:, column % 4 * P : (column % 4 + 1) * P],
-                        in_=z[branch][:, parity * P : (parity + 1) * P],
-                        func=GATE_FUNC[gate],
-                        bias=bias[:, column : column + 1],
-                    )
-
-        def both(name):
-            return keep.tile([P, H], F32, name=name)
-
-        def store_transposed(dram, value, name):
-            bank = flipped.tile([P, BANK], F32, name="bank", tag="bank")
+        def passes(gate, branch):
+            slot = slot_of(gate, branch)
+            z[gate, branch] = sums.tile([P, H], F32, name="z", tag="z")
             for parity in range(PARITIES):
-                nc.tensor.transpose(
-                    bank[:, parity * P : (parity + 1) * P], value[:, parity * P : (parity + 1) * P], ident[:]
+                cols = slice(parity * P, (parity + 1) * P)
+                nc.tensor.matmul_mx(
+                    out=z[gate, branch][:, cols],
+                    lhsT=w_codes[:, slot, cols].bitcast(FP8X4),
+                    lhsT_scale=w_scales[:, slot, cols],
+                    rhs=hx_codes[:, branch * P : (branch + 1) * P].bitcast(FP8X4),
+                    rhs_scale=hx_scales[:, branch * P : (branch + 1) * P],
+                    start=True,
+                    stop=True,
                 )
-            rows = keep.tile([P, H], F32, name=name)
-            nc.scalar.copy(
-                out=rows[:].rearrange("b (m a) -> b m a", a=PARITIES),
-                in_=bank[:, 0:H].rearrange("b (a m) -> b m a", a=PARITIES),
-            )
-            nc.sync.dma_start(out=dram, in_=rows[:])
 
-        flip_weights("i")
-        quantise_weights("i")
+        def activate(gate, branch):
+            for parity in range(PARITIES):
+                column = PARITIES * slot_of(gate, branch) + parity
+                nc.scalar.activation(
+                    out=gate_sb[gate][:, branch * H + parity * P : branch * H + (parity + 1) * P],
+                    in_=z[gate, branch][:, parity * P : (parity + 1) * P],
+                    func=GATE_FUNC[gate],
+                    bias=bias[:, column : column + 1],
+                )
 
-        flip_weights("c")
+        def add_transposed(total, terms, first, last):
+            for branch in range(BRANCHES):
+                for parity in range(PARITIES):
+                    nc.tensor.matmul(
+                        out=total[:, parity * P : (parity + 1) * P],
+                        lhsT=terms[:, branch * H + parity * P : branch * H + (parity + 1) * P],
+                        rhs=ident[:],
+                        start=first and branch == 0 and parity == 0,
+                        stop=last and branch == BRANCHES - 1 and parity == PARITIES - 1,
+                        is_transpose=True,
+                    )
+
+        c_total = totals.tile([P, H], F32, name="c_total")
+        o_total = totals.tile([P, H], F32, name="o_total")
+
+        for branch in range(BRANCHES):
+            prepare("i", branch)
+        for branch in range(BRANCHES):
+            prepare("c", branch)
         flip_biases(0)
-        gate_values("i")
-        quantise_weights("c")
+        for branch in range(BRANCHES):
+            passes("i", branch)
+        for branch in range(BRANCHES):
+            activate("i", branch)
 
-        flip_weights("f")
-        gate_values("c")
-        quantise_weights("f")
-        products = keep.tile([P, BRANCHES * H], F32, name="products")
-        nc.vector.tensor_mul(out=products[:], in0=gate_sb["i"][:], in1=gate_sb["c"][:])
-        written = both("written")
-        nc.vector.tensor_add(out=written[:], in0=products[:, 0:H], in1=products[:, H : 2 * H])
+        for branch in range(BRANCHES):
+            prepare("f", branch)
+        for branch in range(BRANCHES):
+            passes("c", branch)
+        for branch in range(BRANCHES):
+            activate("c", branch)
 
-        flip_weights("o")
+        prepare("o", 0)
+        written = keep.tile([P, BRANCHES * H], F32, name="written")
+        nc.vector.tensor_mul(out=written[:], in0=gate_sb["i"][:], in1=gate_sb["c"][:])
+        prepare("o", 1)
         flip_biases(1)
-        gate_values("f")
-        quantise_weights("o")
-        f_sum = both("f_sum")
-        nc.vector.tensor_add(out=f_sum[:], in0=gate_sb["f"][:, 0:H], in1=gate_sb["f"][:, H : 2 * H])
-        kept = both("kept")
-        nc.vector.tensor_mul(out=kept[:], in0=f_sum[:], in1=c_old[:])
-        c_new = both("c_new")
-        nc.vector.tensor_add(out=c_new[:], in0=kept[:], in1=written[:])
+        cl_bank = flip(words(cl_sb, 0))
+        c_old = keep.tile([P, H], F32, name="c_old")
+        nc.scalar.copy(
+            out=c_old[:].rearrange("m (a b) -> m a b", a=PARITIES),
+            in_=cl_bank[:, 0:P].bitcast(BF16).rearrange("m (b a) -> m a b", a=PARITIES),
+        )
+        for branch in range(BRANCHES):
+            passes("f", branch)
+        for branch in range(BRANCHES):
+            activate("f", branch)
+        add_transposed(c_total, written, True, False)
+        kept = keep.tile([P, BRANCHES * H], F32, name="kept")
+        nc.vector.tensor_mul(
+            out=kept[:].rearrange("m (r n) -> m r n", r=BRANCHES),
+            in0=gate_sb["f"][:].rearrange("m (r n) -> m r n", r=BRANCHES),
+            in1=c_old[:].unsqueeze(1).to_broadcast([P, BRANCHES, H]),
+        )
+        for branch in range(BRANCHES):
+            passes("o", branch)
+            activate("o", branch)
+        add_transposed(c_total, kept, False, True)
 
-        gate_values("o")
-        tanh_c = both("tanh_c")
-        nc.scalar.activation(out=tanh_c[:], in_=c_new[:], func=ACT.Tanh)
-        store_transposed(out_1, c_new, "c_rows")
-        o_sum = both("o_sum")
-        nc.vector.tensor_add(out=o_sum[:], in0=gate_sb["o"][:, 0:H], in1=gate_sb["o"][:, H : 2 * H])
-        h_new = both("h_new")
-        nc.vector.tensor_mul(out=h_new[:], in0=o_sum[:], in1=tanh_c[:])
-        store_transposed(out_0, h_new, "h_rows")
+        tanh_c = keep.tile([P, H], F32, name="tanh_c")
+        nc.scalar.activation(
+            out=tanh_c[:].rearrange("b (m a) -> b m a", a=PARITIES),
+            in_=c_total[:].rearrange("b (a m) -> b m a", a=PARITIES),
+            func=ACT.Tanh,
+        )
+        c_rows = keep.tile([P, H], F32, name="c_rows")
+        nc.scalar.copy(
+            out=c_rows[:].rearrange("b (m a) -> b m a", a=PARITIES),
+            in_=c_total[:].rearrange("b (a m) -> b m a", a=PARITIES),
+        )
+        nc.sync.dma_start(out=out_1, in_=c_rows[:])
+        add_transposed(o_total, gate_sb["o"], True, True)
+        h_rows = keep.tile([P, H], F32, name="h_rows")
+        nc.vector.tensor_mul(
+            out=h_rows[:].rearrange("b (m a) -> b m a", a=PARITIES),
+            in0=o_total[:].rearrange("b (a m) -> b m a", a=PARITIES),
+            in1=tanh_c[:].rearrange("b (m a) -> b m a", a=PARITIES),
+        )
+        nc.sync.dma_start(out=out_0, in_=h_rows[:])

@@ -15,6 +15,7 @@ H = 256
 K = 2 * H
 BRANCHES = 2
 PARITIES = 2
+WARM_UP_PASSES = 12
 GATES = ("i", "c", "f", "o")
 GATE_FUNC = {"i": ACT.Sigmoid, "c": ACT.Tanh, "f": ACT.Sigmoid, "o": ACT.Sigmoid}
 
@@ -67,6 +68,24 @@ def tile_customlstmcell_s_kernel(
         sums = ctx.enter_context(tc.psum_pool(name="sums", bufs=2))
         totals = ctx.enter_context(tc.psum_pool(name="totals", bufs=1))
         ctx.enter_context(tc.manual_schedule())
+
+        c_total = totals.tile([P, H], F32, name="c_total")
+        o_total = totals.tile([P, H], F32, name="o_total")
+        zeros = keep.tile([P, 4 * P], BF16, name="zeros", align_bytes=64)
+        zero_codes = keep.tile([P, P], U32, name="zero_codes", align_bytes=64)
+        zero_scales = keep.tile([P, P], U8, name="zero_scales", align_bytes=64)
+        nc.vector.memset(zeros[:], 0.0)
+        nc.vector.quantize_mx(out=zero_codes[:].bitcast(FP8X4), scales=zero_scales[:], in_=zeros[:])
+        for repeat in range(WARM_UP_PASSES):
+            nc.tensor.matmul_mx(
+                out=o_total[:, 0:P],
+                lhsT=zero_codes[:].bitcast(FP8X4),
+                lhsT_scale=zero_scales[:],
+                rhs=zero_codes[:].bitcast(FP8X4),
+                rhs_scale=zero_scales[:],
+                start=True,
+                stop=True,
+            )
 
         ident = keep.tile([P, P], F32, name="ident")
         make_identity(nc, ident[:])
@@ -212,9 +231,6 @@ def tile_customlstmcell_s_kernel(
                         stop=last and branch == BRANCHES - 1 and parity == PARITIES - 1,
                         is_transpose=True,
                     )
-
-        c_total = totals.tile([P, H], F32, name="c_total")
-        o_total = totals.tile([P, H], F32, name="o_total")
 
         for branch in range(BRANCHES):
             prepare("i", branch)

@@ -15,7 +15,9 @@ H = 256
 K = 2 * H
 BRANCHES = 2
 PARITIES = 2
-WARM_UP_PASSES = 12
+IDLE_AT_START = 10
+IDLE_ALONE = 6
+IDLE_BEHIND_A_GATE = 2
 GATES = ("i", "c", "f", "o")
 GATE_FUNC = {"i": ACT.Sigmoid, "c": ACT.Tanh, "f": ACT.Sigmoid, "o": ACT.Sigmoid}
 
@@ -76,16 +78,20 @@ def tile_customlstmcell_s_kernel(
         zero_scales = keep.tile([P, P], U8, name="zero_scales", align_bytes=64)
         nc.vector.memset(zeros[:], 0.0)
         nc.vector.quantize_mx(out=zero_codes[:].bitcast(FP8X4), scales=zero_scales[:], in_=zeros[:])
-        for repeat in range(WARM_UP_PASSES):
-            nc.tensor.matmul_mx(
-                out=o_total[:, 0:P],
-                lhsT=zero_codes[:].bitcast(FP8X4),
-                lhsT_scale=zero_scales[:],
-                rhs=zero_codes[:].bitcast(FP8X4),
-                rhs_scale=zero_scales[:],
-                start=True,
-                stop=True,
-            )
+
+        def idle_passes(count):
+            for repeat in range(count):
+                nc.tensor.matmul_mx(
+                    out=o_total[:, 0:P],
+                    lhsT=zero_codes[:].bitcast(FP8X4),
+                    lhsT_scale=zero_scales[:],
+                    rhs=zero_codes[:].bitcast(FP8X4),
+                    rhs_scale=zero_scales[:],
+                    start=True,
+                    stop=True,
+                )
+
+        idle_passes(IDLE_AT_START)
 
         ident = keep.tile([P, P], F32, name="ident")
         make_identity(nc, ident[:])
@@ -234,11 +240,13 @@ def tile_customlstmcell_s_kernel(
 
         for branch in range(BRANCHES):
             prepare("i", branch)
+        idle_passes(IDLE_ALONE)
         for branch in range(BRANCHES):
             prepare("c", branch)
         flip_biases(0)
         for branch in range(BRANCHES):
             passes("i", branch)
+        idle_passes(IDLE_BEHIND_A_GATE)
         for branch in range(BRANCHES):
             activate("i", branch)
 
@@ -246,6 +254,7 @@ def tile_customlstmcell_s_kernel(
             prepare("f", branch)
         for branch in range(BRANCHES):
             passes("c", branch)
+        idle_passes(IDLE_BEHIND_A_GATE)
         for branch in range(BRANCHES):
             activate("c", branch)
 
@@ -262,6 +271,7 @@ def tile_customlstmcell_s_kernel(
         )
         for branch in range(BRANCHES):
             passes("f", branch)
+        idle_passes(IDLE_BEHIND_A_GATE)
         for branch in range(BRANCHES):
             activate("f", branch)
         add_transposed(c_total, written, True, False)

from contextlib import ExitStack

import concourse.mybir as mybir
from concourse.masks import make_identity

BF16 = mybir.dt.bfloat16
F32 = mybir.dt.float32
U32 = mybir.dt.uint32
U8 = mybir.dt.uint8
FP8X4 = mybir.dt.float8_e4m3fn_x4
ACT = mybir.ActivationFunctionType

P = 128
H = 256
K = 2 * H
BRANCHES = 2
PARITIES = 2
IDLE_AT_START = 10
IDLE_ALONE = 6
IDLE_BEHIND_A_GATE = 2
GATES = ("i", "c", "f", "o")
GATE_FUNC = {"i": ACT.Sigmoid, "c": ACT.Tanh, "f": ACT.Sigmoid, "o": ACT.Sigmoid}

FLOPS = 2 * P * K * len(GATES) * BRANCHES * H


def tile_customlstmcell_s_kernel(
    tc,
    y,
    h_light,
    c_light,
    h_temp,
    c_temp,
    w_f_light,
    b_f_light,
    w_i_light,
    b_i_light,
    w_c_light,
    b_c_light,
    w_o_light,
    b_o_light,
    w_f_light_temp,
    b_f_light_temp,
    w_i_light_temp,
    b_i_light_temp,
    w_c_light_temp,
    b_c_light_temp,
    w_o_light_temp,
    b_o_light_temp,
    out_0,
    out_1,
):
    nc = tc.nc
    weight_of = {
        "f": (w_f_light, w_f_light_temp),
        "i": (w_i_light, w_i_light_temp),
        "c": (w_c_light, w_c_light_temp),
        "o": (w_o_light, w_o_light_temp),
    }
    bias_of = {
        "f": (b_f_light, b_f_light_temp),
        "i": (b_i_light, b_i_light_temp),
        "c": (b_c_light, b_c_light_temp),
        "o": (b_o_light, b_o_light_temp),
    }

    with ExitStack() as ctx:
        keep = ctx.enter_context(tc.tile_pool(name="keep", bufs=1))
        flipped = ctx.enter_context(tc.psum_pool(name="flipped", bufs=4))
        sums = ctx.enter_context(tc.psum_pool(name="sums", bufs=2))
        totals = ctx.enter_context(tc.psum_pool(name="totals", bufs=1))
        ctx.enter_context(tc.manual_schedule())

        c_total = totals.tile([P, H], F32, name="c_total")
        o_total = totals.tile([P, H], F32, name="o_total")
        zeros = keep.tile([P, 4 * P], BF16, name="zeros", align_bytes=64)
        zero_codes = keep.tile([P, P], U32, name="zero_codes", align_bytes=64)
        zero_scales = keep.tile([P, P], U8, name="zero_scales", align_bytes=64)
        nc.vector.memset(zeros[:], 0.0)
        nc.vector.quantize_mx(out=zero_codes[:].bitcast(FP8X4), scales=zero_scales[:], in_=zeros[:])

        def idle_passes(count):
            for repeat in range(count):
                nc.tensor.matmul_mx(
                    out=o_total[:, 0:P],
                    lhsT=zero_codes[:].bitcast(FP8X4),
                    lhsT_scale=zero_scales[:],
                    rhs=zero_codes[:].bitcast(FP8X4),
                    rhs_scale=zero_scales[:],
                    start=True,
                    stop=True,
                )

        idle_passes(IDLE_AT_START)

        ident = keep.tile([P, P], F32, name="ident")
        make_identity(nc, ident[:])
        bias_rows = [keep.tile([P, H], BF16, name="bias_rows_%d" % half) for half in range(2)]
        for half in range(2):
            nc.vector.memset(bias_rows[half][:], 0.0)
        warm_in = keep.tile([P, 1], F32, name="warm_in")
        warm_out = keep.tile([P, 1], F32, name="warm_out")
        nc.vector.memset(warm_in[:], 0.0)
        nc.scalar.activation(out=warm_out[:], in_=warm_in[:], func=ACT.Sigmoid)

        hl_sb = keep.tile([P, H], BF16, name="hl_sb")
        y_sb = keep.tile([P, H], BF16, name="y_sb")
        ht_sb = keep.tile([P, H], BF16, name="ht_sb")
        cl_sb = keep.tile([P, H], BF16, name="cl_sb")
        w_sb = {}
        for gate in GATES:
            for branch in range(BRANCHES):
                w_sb[gate, branch] = keep.tile([P, PARITIES * K], BF16, name="w_%s%d" % (gate, branch))

        def load_weights(gate):
            for branch in range(BRANCHES):
                nc.sync.dma_start(
                    out=w_sb[gate, branch][:],
                    in_=weight_of[gate][branch].rearrange("(m a) k -> m (a k)", a=PARITIES),
                )

        def load_biases(half):
            for place, gate in enumerate(GATES[2 * half : 2 * half + 2]):
                for branch in range(BRANCHES):
                    row = BRANCHES * place + branch
                    nc.sync.dma_start(
                        out=bias_rows[half][row : row + 1, :],
                        in_=bias_of[gate][branch].rearrange("(o n) -> o n", o=1),
                    )

        nc.sync.dma_start(out=hl_sb[:], in_=h_light)
        nc.sync.dma_start(out=y_sb[:], in_=y)
        nc.sync.dma_start(out=ht_sb[:], in_=h_temp)
        load_weights("i")
        load_weights("c")
        load_biases(0)
        load_weights("f")
        load_weights("o")
        load_biases(1)
        nc.sync.dma_start(out=cl_sb[:], in_=c_light)

        def words(tile_bf16, first_word):
            return tile_bf16[:].bitcast(F32)[:, first_word : first_word + P]

        def flip(*sources):
            bank = flipped.tile([P, 2 * P], F32, name="bank", tag="bank")
            for u, source in enumerate(sources):
                nc.tensor.transpose(bank[:, u * P : (u + 1) * P], source, ident[:])
            return bank

        def quantise(second, bank, codes, scales, name):
            grouped = keep.tile([P, 4 * P], BF16, name=name, align_bytes=64)
            src = bank[:].rearrange("q (u r) -> q r u", u=2)
            dst = grouped[:].bitcast(F32).rearrange("q (r u) -> q r u", u=2)
            if second:
                nc.vector.tensor_copy(out=dst, in_=src)
            else:
                nc.scalar.copy(out=dst, in_=src)
            return lambda: nc.vector.quantize_mx(out=codes.bitcast(FP8X4), scales=scales, in_=grouped[:])

        def halves(pair_of_sources, codes, scales, name):
            pending = []
            for second, sources in enumerate(pair_of_sources):
                cols = slice(second * P, (second + 1) * P)
                bank = flip(*sources)
                pending.append(quantise(second, bank, codes[:, cols], scales[:, cols], "%s%d" % (name, second)))
            for issue in pending:
                issue()

        hx_codes = keep.tile([P, BRANCHES * P], U32, name="hx_codes", align_bytes=64)
        hx_scales = keep.tile([P, BRANCHES * P], U8, name="hx_scales", align_bytes=64)
        halves(
            ((words(hl_sb, 0), words(y_sb, 0)), (words(ht_sb, 0), words(y_sb, 0))),
            hx_codes[:],
            hx_scales[:],
            "hx_grouped",
        )

        w_codes = keep.tile([P, len(GATES) * BRANCHES, H], U32, name="w_codes", align_bytes=64)
        w_scales = keep.tile([P, len(GATES) * BRANCHES, H], U8, name="w_scales", align_bytes=64)
        bias = keep.tile([P, len(GATES) * BRANCHES * PARITIES], F32, name="bias")
        gate_sb = {}
        for gate in GATES:
            gate_sb[gate] = keep.tile([P, BRANCHES * H], F32, name="gate_%s" % gate)
        z = {}

        def slot_of(gate, branch):
            return BRANCHES * GATES.index(gate) + branch

        def prepare(gate, branch):
            tile_bf16 = w_sb[gate, branch]
            slot = slot_of(gate, branch)
            halves(
                [(words(tile_bf16, parity * H), words(tile_bf16, parity * H + P)) for parity in range(PARITIES)],
                w_codes[:, slot, :],
                w_scales[:, slot, :],
                "grouped_%s%d" % (gate, branch),
            )

        def flip_biases(half):
            bank = flip(words(bias_rows[half], 0))
            nc.scalar.copy(out=bias[:, 8 * half : 8 * half + 8], in_=bank[:, 0:4].bitcast(BF16))

        def passes(gate, branch):
            slot = slot_of(gate, branch)
            z[gate, branch] = sums.tile([P, H], F32, name="z", tag="z")
            for parity in range(PARITIES):
                cols = slice(parity * P, (parity + 1) * P)
                nc.tensor.matmul_mx(
                    out=z[gate, branch][:, cols],
                    lhsT=w_codes[:, slot, cols].bitcast(FP8X4),
                    lhsT_scale=w_scales[:, slot, cols],
                    rhs=hx_codes[:, branch * P : (branch + 1) * P].bitcast(FP8X4),
                    rhs_scale=hx_scales[:, branch * P : (branch + 1) * P],
                    start=True,
                    stop=True,
                )

        def activate(gate, branch):
            for parity in range(PARITIES):
                column = PARITIES * slot_of(gate, branch) + parity
                nc.scalar.activation(
                    out=gate_sb[gate][:, branch * H + parity * P : branch * H + (parity + 1) * P],
                    in_=z[gate, branch][:, parity * P : (parity + 1) * P],
                    func=GATE_FUNC[gate],
                    bias=bias[:, column : column + 1],
                )

        def add_transposed(total, terms, first, last):
            for branch in range(BRANCHES):
                for parity in range(PARITIES):
                    nc.tensor.matmul(
                        out=total[:, parity * P : (parity + 1) * P],
                        lhsT=terms[:, branch * H + parity * P : branch * H + (parity + 1) * P],
                        rhs=ident[:],
                        start=first and branch == 0 and parity == 0,
                        stop=last and branch == BRANCHES - 1 and parity == PARITIES - 1,
                        is_transpose=True,
                    )

        for branch in range(BRANCHES):
            prepare("i", branch)
        idle_passes(IDLE_ALONE)
        for branch in range(BRANCHES):
            prepare("c", branch)
        flip_biases(0)
        for branch in range(BRANCHES):
            passes("i", branch)
        idle_passes(IDLE_BEHIND_A_GATE)
        for branch in range(BRANCHES):
            activate("i", branch)

        for branch in range(BRANCHES):
            prepare("f", branch)
        for branch in range(BRANCHES):
            passes("c", branch)
        idle_passes(IDLE_BEHIND_A_GATE)
        for branch in range(BRANCHES):
            activate("c", branch)

        prepare("o", 0)
        written = keep.tile([P, BRANCHES * H], F32, name="written")
        nc.vector.tensor_mul(out=written[:], in0=gate_sb["i"][:], in1=gate_sb["c"][:])
        prepare("o", 1)
        flip_biases(1)
        cl_bank = flip(words(cl_sb, 0))
        c_old = keep.tile([P, H], F32, name="c_old")
        nc.scalar.copy(
            out=c_old[:].rearrange("m (a b) -> m a b", a=PARITIES),
            in_=cl_bank[:, 0:P].bitcast(BF16).rearrange("m (b a) -> m a b", a=PARITIES),
        )
        for branch in range(BRANCHES):
            passes("f", branch)
        idle_passes(IDLE_BEHIND_A_GATE)
        for branch in range(BRANCHES):
            activate("f", branch)
        add_transposed(c_total, written, True, False)
        kept = keep.tile([P, BRANCHES * H], F32, name="kept")
        nc.vector.tensor_mul(
            out=kept[:].rearrange("m (r n) -> m r n", r=BRANCHES),
            in0=gate_sb["f"][:].rearrange("m (r n) -> m r n", r=BRANCHES),
            in1=c_old[:].unsqueeze(1).to_broadcast([P, BRANCHES, H]),
        )
        for branch in range(BRANCHES):
            passes("o", branch)
            activate("o", branch)
        add_transposed(c_total, kept, False, True)

        tanh_c = keep.tile([P, H], F32, name="tanh_c")
        nc.scalar.activation(
            out=tanh_c[:].rearrange("b (m a) -> b m a", a=PARITIES),
            in_=c_total[:].rearrange("b (a m) -> b m a", a=PARITIES),
            func=ACT.Tanh,
        )
        c_rows = keep.tile([P, H], F32, name="c_rows")
        nc.scalar.copy(
            out=c_rows[:].rearrange("b (m a) -> b m a", a=PARITIES),
            in_=c_total[:].rearrange("b (a m) -> b m a", a=PARITIES),
        )
        nc.sync.dma_start(out=out_1, in_=c_rows[:])
        add_transposed(o_total, gate_sb["o"], True, True)
        h_rows = keep.tile([P, H], F32, name="h_rows")
        nc.vector.tensor_mul(
            out=h_rows[:].rearrange("b (m a) -> b m a", a=PARITIES),
            in0=o_total[:].rearrange("b (a m) -> b m a", a=PARITIES),
            in1=tanh_c[:].rearrange("b (m a) -> b m a", a=PARITIES),
        )
        nc.sync.dma_start(out=out_0, in_=h_rows[:])
